import numpy as np
import ml_dtypes

BF16 = ml_dtypes.bfloat16


def bf(x):
    return np.asarray(x, np.float32).astype(BF16)


def f32(x):
    return np.asarray(x, np.float32)


def f64(x):
    return np.asarray(x).astype(np.float64)


def striped(idx):
    return np.tile(idx.reshape(-1, 16).T, (8, 1))


R, NN, K, C, NIN, S, N = 2, 32, 8, 128, 384, 2048, 512


def setup_inputs():
    idx = np.concatenate([row * NN + np.random.permutation(NN)[:K] for row in range(R * NN)])
    return {
        "base": f32(np.random.standard_normal((C, S))),
        "h_ev": bf(np.random.standard_normal((NIN, N))),
        "w1": bf(np.random.standard_normal((NIN, C)) / np.sqrt(NIN)),
        "b1": f32(0.1 * np.random.standard_normal((C, 1))),
        "w3": bf(np.random.standard_normal((C, C)) * np.sqrt(2.0 / C)),
        "b3": f32(0.1 * np.random.standard_normal((C, 1))),
        "offs": striped(idx),
    }


def reference(base, h_ev, w1, b1, w3, b3, offs):
    idx = offs[:16].T.reshape(-1)
    hid = np.maximum(f64(w1).T @ f64(h_ev) + f64(b1), 0.0)
    out = f64(base).copy()
    out[:, idx] = f64(w3).T @ hid + f64(b3)
    return out

@@ -1,0 +1,63 @@
+import concourse.mybir as mybir
+
+P = 128
+N_EDGES = 512
+N_PLACES = 2048
+K_BLOCKS = 3
+
+FLOPS = 2 * K_BLOCKS * P * P * N_EDGES + 2 * P * P * N_EDGES
+
+BF16, F32, U16 = mybir.dt.bfloat16, mybir.dt.float32, mybir.dt.uint16
+ADD, MAX, MULT = mybir.AluOpType.add, mybir.AluOpType.max, mybir.AluOpType.mult
+
+
+def tile_termedgempnnlayer_s_kernel(tc, base, h_ev, w1, b1, w3, b3, offs, out):
+    nc = tc.nc
+    half = N_PLACES // 2
+    with (
+        tc.tile_pool(name="held", bufs=1) as held,
+        tc.psum_pool(name="psum", bufs=1) as psum,
+    ):
+        offsets = held.tile([P, N_EDGES // 16], U16, name="offsets")
+        nc.sync.dma_start(offsets[:], offs)
+
+        w1_sb = held.tile([P, K_BLOCKS, P], BF16, name="w1_sb")
+        nc.scalar.dma_start(w1_sb[:], w1.rearrange("(k p) h -> p k h", p=P))
+        edges = []
+        for k in range(K_BLOCKS):
+            block = held.tile([P, N_EDGES], BF16, name=f"edges{k}")
+            nc.sync.dma_start(block[:], h_ev[k * P : (k + 1) * P, :])
+            edges.append(block)
+        b1_sb = held.tile([P, 1], F32, name="b1_sb")
+        nc.scalar.dma_start(b1_sb[:], b1)
+        w3_sb = held.tile([P, P], BF16, name="w3_sb")
+        nc.scalar.dma_start(w3_sb[:], w3)
+        b3_sb = held.tile([P, 1], F32, name="b3_sb")
+        nc.scalar.dma_start(b3_sb[:], b3)
+
+        b3_wide = held.tile([P, N_EDGES], F32, name="b3_wide")
+        nc.gpsimd.memset(b3_wide[:], 0.0)
+        nc.gpsimd.tensor_scalar(b3_wide[:], b3_wide[:], 1.0, b3_sb[:, 0:1], MULT, ADD)
+
+        window = held.tile([P, N_PLACES], F32, name="window")
+        nc.sync.dma_start(window[:, :half], base[:, :half])
+        nc.scalar.dma_start(window[:, half:], base[:, half:])
+
+        hid_ps = psum.tile([P, N_EDGES], F32, name="hid_ps")
+        for k in range(K_BLOCKS):
+            nc.tensor.matmul(
+                hid_ps[:], w1_sb[:, k, :], edges[k][:], start=(k == 0), stop=(k == K_BLOCKS - 1)
+            )
+        hid = held.tile([P, N_EDGES], BF16, name="hid")
+        nc.vector.tensor_scalar(hid[:], hid_ps[:], b1_sb[:, 0:1], 0.0, ADD, MAX)
+
+        msg_ps = psum.tile([P, N_EDGES], F32, name="msg_ps")
+        nc.tensor.matmul(msg_ps[:], w3_sb[:], hid[:], start=True, stop=True)
+
+        msg = held.tile([P, N_EDGES], F32, name="msg")
+        nc.vector.tensor_copy(msg[:], msg_ps[:])
+
+        nc.vector.tensor_tensor(window[:].indirect(offsets[:]), msg[:], b3_wide[:], ADD)
+
+        nc.sync.dma_start(out[:, :half], window[:, :half])
+        nc.scalar.dma_start(out[:, half:], window[:, half:])

@@ -4,6 +4,8 @@ P = 128
 N_EDGES = 512
 N_PLACES = 2048
 K_BLOCKS = 3
+N_CHUNKS = 2
+CHUNK = N_EDGES // N_CHUNKS
 
 FLOPS = 2 * K_BLOCKS * P * P * N_EDGES + 2 * P * P * N_EDGES
 
@@ -43,19 +45,24 @@ def tile_termedgempnnlayer_s_kernel(tc, base, h_ev, w1, b1, w3, b3, offs, out):
         nc.sync.dma_start(window[:, :half], base[:, :half])
         nc.scalar.dma_start(window[:, half:], base[:, half:])
 
-        hid_ps = psum.tile([P, N_EDGES], F32, name="hid_ps")
-        for k in range(K_BLOCKS):
-            nc.tensor.matmul(
-                hid_ps[:], w1_sb[:, k, :], edges[k][:], start=(k == 0), stop=(k == K_BLOCKS - 1)
-            )
-        hid = held.tile([P, N_EDGES], BF16, name="hid")
-        nc.vector.tensor_scalar(hid[:], hid_ps[:], b1_sb[:, 0:1], 0.0, ADD, MAX)
-
-        msg_ps = psum.tile([P, N_EDGES], F32, name="msg_ps")
-        nc.tensor.matmul(msg_ps[:], w3_sb[:], hid[:], start=True, stop=True)
+        hid = []
+        for c in range(N_CHUNKS):
+            cols = slice(c * CHUNK, (c + 1) * CHUNK)
+            hid_ps = psum.tile([P, CHUNK], F32, name=f"hid_ps{c}")
+            for k in range(K_BLOCKS):
+                nc.tensor.matmul(
+                    hid_ps[:], w1_sb[:, k, :], edges[k][:, cols], start=(k == 0), stop=(k == K_BLOCKS - 1)
+                )
+            hid_c = held.tile([P, CHUNK], BF16, name=f"hid{c}")
+            nc.vector.tensor_scalar(hid_c[:], hid_ps[:], b1_sb[:, 0:1], 0.0, ADD, MAX)
+            hid.append(hid_c)
 
         msg = held.tile([P, N_EDGES], F32, name="msg")
-        nc.vector.tensor_copy(msg[:], msg_ps[:])
+        for c in range(N_CHUNKS):
+            cols = slice(c * CHUNK, (c + 1) * CHUNK)
+            msg_ps = psum.tile([P, CHUNK], F32, name=f"msg_ps{c}")
+            nc.tensor.matmul(msg_ps[:], w3_sb[:], hid[c][:], start=True, stop=True)
+            nc.vector.tensor_copy(msg[:, cols], msg_ps[:])
 
         nc.vector.tensor_tensor(window[:].indirect(offsets[:]), msg[:], b3_wide[:], ADD)
 

@@ -6,6 +6,7 @@ N_PLACES = 2048
 K_BLOCKS = 3
 N_CHUNKS = 2
 CHUNK = N_EDGES // N_CHUNKS
+WARM_MATMULS = 6
 
 FLOPS = 2 * K_BLOCKS * P * P * N_EDGES + 2 * P * P * N_EDGES
 
@@ -44,6 +45,12 @@ def tile_termedgempnnlayer_s_kernel(tc, base, h_ev, w1, b1, w3, b3, offs, out):
         window = held.tile([P, N_PLACES], F32, name="window")
         nc.sync.dma_start(window[:, :half], base[:, :half])
         nc.scalar.dma_start(window[:, half:], base[:, half:])
+
+        zeros = held.tile([P, N_EDGES], BF16, name="zeros")
+        nc.vector.memset(zeros[:], 0.0)
+        warm_ps = psum.tile([P, N_EDGES], F32, name="warm_ps")
+        for i in range(WARM_MATMULS):
+            nc.tensor.matmul(warm_ps[:], zeros[:, :P], zeros[:], start=True, stop=True)
 
         hid = []
         for c in range(N_CHUNKS):

@@ -12,6 +12,7 @@ FLOPS = 2 * K_BLOCKS * P * P * N_EDGES + 2 * P * P * N_EDGES
 
 BF16, F32, U16 = mybir.dt.bfloat16, mybir.dt.float32, mybir.dt.uint16
 ADD, MAX, MULT = mybir.AluOpType.add, mybir.AluOpType.max, mybir.AluOpType.mult
+RELU, COPY = mybir.ActivationFunctionType.Relu, mybir.ActivationFunctionType.Copy
 
 
 def tile_termedgempnnlayer_s_kernel(tc, base, h_ev, w1, b1, w3, b3, offs, out):
@@ -21,55 +22,53 @@ def tile_termedgempnnlayer_s_kernel(tc, base, h_ev, w1, b1, w3, b3, offs, out):
         tc.tile_pool(name="held", bufs=1) as held,
         tc.psum_pool(name="psum", bufs=1) as psum,
     ):
-        offsets = held.tile([P, N_EDGES // 16], U16, name="offsets")
-        nc.sync.dma_start(offsets[:], offs)
+        zeros = held.tile([P, CHUNK], BF16, name="zeros")
+        nc.vector.memset(zeros[:], 0.0)
+        warm_ps = psum.tile([P, CHUNK], F32, name="warm_ps")
+        for i in range(WARM_MATMULS):
+            nc.tensor.matmul(warm_ps[:], zeros[:, :P], zeros[:], start=True, stop=True)
 
         w1_sb = held.tile([P, K_BLOCKS, P], BF16, name="w1_sb")
-        nc.scalar.dma_start(w1_sb[:], w1.rearrange("(k p) h -> p k h", p=P))
-        edges = []
-        for k in range(K_BLOCKS):
-            block = held.tile([P, N_EDGES], BF16, name=f"edges{k}")
-            nc.sync.dma_start(block[:], h_ev[k * P : (k + 1) * P, :])
-            edges.append(block)
+        nc.scalar.dma_start(w1_sb[:], w1.rearrange("(p k) h -> p k h", k=K_BLOCKS))
+        edges = held.tile([P, K_BLOCKS, N_EDGES], BF16, name="edges")
+        nc.sync.dma_start(edges[:], h_ev.rearrange("(p k) j -> p k j", k=K_BLOCKS))
         b1_sb = held.tile([P, 1], F32, name="b1_sb")
         nc.scalar.dma_start(b1_sb[:], b1)
+        b3_sb = held.tile([P, 1], F32, name="b3_sb")
+        nc.sync.dma_start(b3_sb[:], b3)
         w3_sb = held.tile([P, P], BF16, name="w3_sb")
         nc.scalar.dma_start(w3_sb[:], w3)
-        b3_sb = held.tile([P, 1], F32, name="b3_sb")
-        nc.scalar.dma_start(b3_sb[:], b3)
+        offsets = held.tile([P, N_EDGES // 16], U16, name="offsets")
+        nc.sync.dma_start(offsets[:], offs)
+        window = held.tile([P, N_PLACES], F32, name="window")
+        nc.sync.dma_start(window[:, :half], base[:, :half])
+        nc.scalar.dma_start(window[:, half:], base[:, half:])
 
         b3_wide = held.tile([P, N_EDGES], F32, name="b3_wide")
         nc.gpsimd.memset(b3_wide[:], 0.0)
         nc.gpsimd.tensor_scalar(b3_wide[:], b3_wide[:], 1.0, b3_sb[:, 0:1], MULT, ADD)
 
-        window = held.tile([P, N_PLACES], F32, name="window")
-        nc.sync.dma_start(window[:, :half], base[:, :half])
-        nc.scalar.dma_start(window[:, half:], base[:, half:])
-
-        zeros = held.tile([P, N_EDGES], BF16, name="zeros")
-        nc.vector.memset(zeros[:], 0.0)
-        warm_ps = psum.tile([P, N_EDGES], F32, name="warm_ps")
-        for i in range(WARM_MATMULS):
-            nc.tensor.matmul(warm_ps[:], zeros[:, :P], zeros[:], start=True, stop=True)
-
-        hid = []
-        for c in range(N_CHUNKS):
-            cols = slice(c * CHUNK, (c + 1) * CHUNK)
-            hid_ps = psum.tile([P, CHUNK], F32, name=f"hid_ps{c}")
-            for k in range(K_BLOCKS):
+        hid_ps = [psum.tile([P, CHUNK], F32, name=f"hid_ps{c}") for c in range(N_CHUNKS)]
+        for k in range(K_BLOCKS):
+            for c in range(N_CHUNKS):
                 nc.tensor.matmul(
-                    hid_ps[:], w1_sb[:, k, :], edges[k][:, cols], start=(k == 0), stop=(k == K_BLOCKS - 1)
+                    hid_ps[c][:],
+                    w1_sb[:, k, :],
+                    edges[:, k, c * CHUNK : (c + 1) * CHUNK],
+                    start=(k == 0),
+                    stop=(k == K_BLOCKS - 1),
                 )
-            hid_c = held.tile([P, CHUNK], BF16, name=f"hid{c}")
-            nc.vector.tensor_scalar(hid_c[:], hid_ps[:], b1_sb[:, 0:1], 0.0, ADD, MAX)
-            hid.append(hid_c)
 
-        msg = held.tile([P, N_EDGES], F32, name="msg")
+        hid = [held.tile([P, CHUNK], BF16, name=f"hid{c}") for c in range(N_CHUNKS)]
+        nc.scalar.activation(hid[0][:], hid_ps[0][:], RELU, bias=b1_sb[:, 0:1])
+        nc.vector.tensor_scalar(hid[1][:], hid_ps[1][:], b1_sb[:, 0:1], 0.0, ADD, MAX)
+
+        msg_ps = [psum.tile([P, CHUNK], F32, name=f"msg_ps{c}") for c in range(N_CHUNKS)]
         for c in range(N_CHUNKS):
-            cols = slice(c * CHUNK, (c + 1) * CHUNK)
-            msg_ps = psum.tile([P, CHUNK], F32, name=f"msg_ps{c}")
-            nc.tensor.matmul(msg_ps[:], w3_sb[:], hid[c][:], start=True, stop=True)
-            nc.vector.tensor_copy(msg[:, cols], msg_ps[:])
+            nc.tensor.matmul(msg_ps[c][:], w3_sb[:], hid[c][:], start=True, stop=True)
+        msg = held.tile([P, N_EDGES], F32, name="msg")
+        nc.scalar.activation(msg[:, :CHUNK], msg_ps[0][:], COPY)
+        nc.vector.tensor_copy(msg[:, CHUNK:], msg_ps[1][:])
 
         nc.vector.tensor_tensor(window[:].indirect(offsets[:]), msg[:], b3_wide[:], ADD)
 

@@ -12,7 +12,6 @@ FLOPS = 2 * K_BLOCKS * P * P * N_EDGES + 2 * P * P * N_EDGES
 
 BF16, F32, U16 = mybir.dt.bfloat16, mybir.dt.float32, mybir.dt.uint16
 ADD, MAX, MULT = mybir.AluOpType.add, mybir.AluOpType.max, mybir.AluOpType.mult
-RELU, COPY = mybir.ActivationFunctionType.Relu, mybir.ActivationFunctionType.Copy
 
 
 def tile_termedgempnnlayer_s_kernel(tc, base, h_ev, w1, b1, w3, b3, offs, out):
@@ -28,25 +27,31 @@ def tile_termedgempnnlayer_s_kernel(tc, base, h_ev, w1, b1, w3, b3, offs, out):
         for i in range(WARM_MATMULS):
             nc.tensor.matmul(warm_ps[:], zeros[:, :P], zeros[:], start=True, stop=True)
 
-        w1_sb = held.tile([P, K_BLOCKS, P], BF16, name="w1_sb")
-        nc.scalar.dma_start(w1_sb[:], w1.rearrange("(p k) h -> p k h", k=K_BLOCKS))
-        edges = held.tile([P, K_BLOCKS, N_EDGES], BF16, name="edges")
-        nc.sync.dma_start(edges[:], h_ev.rearrange("(p k) j -> p k j", k=K_BLOCKS))
-        b1_sb = held.tile([P, 1], F32, name="b1_sb")
-        nc.scalar.dma_start(b1_sb[:], b1)
-        b3_sb = held.tile([P, 1], F32, name="b3_sb")
-        nc.sync.dma_start(b3_sb[:], b3)
-        w3_sb = held.tile([P, P], BF16, name="w3_sb")
-        nc.scalar.dma_start(w3_sb[:], w3)
         offsets = held.tile([P, N_EDGES // 16], U16, name="offsets")
         nc.sync.dma_start(offsets[:], offs)
-        window = held.tile([P, N_PLACES], F32, name="window")
-        nc.sync.dma_start(window[:, :half], base[:, :half])
-        nc.scalar.dma_start(window[:, half:], base[:, half:])
+
+        w1_sb = held.tile([P, K_BLOCKS, P], BF16, name="w1_sb")
+        nc.scalar.dma_start(w1_sb[:], w1.rearrange("(k p) h -> p k h", p=P))
+        edges = []
+        for k in range(K_BLOCKS):
+            block = held.tile([P, N_EDGES], BF16, name=f"edges{k}")
+            queue = nc.sync if k % 2 == 0 else nc.scalar
+            queue.dma_start(block[:], h_ev[k * P : (k + 1) * P, :])
+            edges.append(block)
+        b1_sb = held.tile([P, 1], F32, name="b1_sb")
+        nc.scalar.dma_start(b1_sb[:], b1)
+        w3_sb = held.tile([P, P], BF16, name="w3_sb")
+        nc.scalar.dma_start(w3_sb[:], w3)
+        b3_sb = held.tile([P, 1], F32, name="b3_sb")
+        nc.scalar.dma_start(b3_sb[:], b3)
 
         b3_wide = held.tile([P, N_EDGES], F32, name="b3_wide")
         nc.gpsimd.memset(b3_wide[:], 0.0)
         nc.gpsimd.tensor_scalar(b3_wide[:], b3_wide[:], 1.0, b3_sb[:, 0:1], MULT, ADD)
+
+        window = held.tile([P, N_PLACES], F32, name="window")
+        nc.sync.dma_start(window[:, :half], base[:, :half])
+        nc.scalar.dma_start(window[:, half:], base[:, half:])
 
         hid_ps = [psum.tile([P, CHUNK], F32, name=f"hid_ps{c}") for c in range(N_CHUNKS)]
         for k in range(K_BLOCKS):
@@ -54,21 +59,22 @@ def tile_termedgempnnlayer_s_kernel(tc, base, h_ev, w1, b1, w3, b3, offs, out):
                 nc.tensor.matmul(
                     hid_ps[c][:],
                     w1_sb[:, k, :],
-                    edges[:, k, c * CHUNK : (c + 1) * CHUNK],
+                    edges[k][:, c * CHUNK : (c + 1) * CHUNK],
                     start=(k == 0),
                     stop=(k == K_BLOCKS - 1),
                 )
-
-        hid = [held.tile([P, CHUNK], BF16, name=f"hid{c}") for c in range(N_CHUNKS)]
-        nc.scalar.activation(hid[0][:], hid_ps[0][:], RELU, bias=b1_sb[:, 0:1])
-        nc.vector.tensor_scalar(hid[1][:], hid_ps[1][:], b1_sb[:, 0:1], 0.0, ADD, MAX)
-
-        msg_ps = [psum.tile([P, CHUNK], F32, name=f"msg_ps{c}") for c in range(N_CHUNKS)]
+        hid = []
         for c in range(N_CHUNKS):
-            nc.tensor.matmul(msg_ps[c][:], w3_sb[:], hid[c][:], start=True, stop=True)
+            hid_c = held.tile([P, CHUNK], BF16, name=f"hid{c}")
+            nc.vector.tensor_scalar(hid_c[:], hid_ps[c][:], b1_sb[:, 0:1], 0.0, ADD, MAX)
+            hid.append(hid_c)
+
         msg = held.tile([P, N_EDGES], F32, name="msg")
-        nc.scalar.activation(msg[:, :CHUNK], msg_ps[0][:], COPY)
-        nc.vector.tensor_copy(msg[:, CHUNK:], msg_ps[1][:])
+        for c in range(N_CHUNKS):
+            cols = slice(c * CHUNK, (c + 1) * CHUNK)
+            msg_ps = psum.tile([P, CHUNK], F32, name=f"msg_ps{c}")
+            nc.tensor.matmul(msg_ps[:], w3_sb[:], hid[c][:], start=True, stop=True)
+            nc.vector.tensor_copy(msg[:, cols], msg_ps[:])
 
         nc.vector.tensor_tensor(window[:].indirect(offsets[:]), msg[:], b3_wide[:], ADD)
 

@@ -6,7 +6,6 @@ N_PLACES = 2048
 K_BLOCKS = 3
 N_CHUNKS = 2
 CHUNK = N_EDGES // N_CHUNKS
-WARM_MATMULS = 6
 
 FLOPS = 2 * K_BLOCKS * P * P * N_EDGES + 2 * P * P * N_EDGES
 
@@ -21,12 +20,6 @@ def tile_termedgempnnlayer_s_kernel(tc, base, h_ev, w1, b1, w3, b3, offs, out):
         tc.tile_pool(name="held", bufs=1) as held,
         tc.psum_pool(name="psum", bufs=1) as psum,
     ):
-        zeros = held.tile([P, CHUNK], BF16, name="zeros")
-        nc.vector.memset(zeros[:], 0.0)
-        warm_ps = psum.tile([P, CHUNK], F32, name="warm_ps")
-        for i in range(WARM_MATMULS):
-            nc.tensor.matmul(warm_ps[:], zeros[:, :P], zeros[:], start=True, stop=True)
-
         offsets = held.tile([P, N_EDGES // 16], U16, name="offsets")
         nc.sync.dma_start(offsets[:], offs)
 

@@ -6,6 +6,7 @@ N_PLACES = 2048
 K_BLOCKS = 3
 N_CHUNKS = 2
 CHUNK = N_EDGES // N_CHUNKS
+WARM_MATMULS = 6
 
 FLOPS = 2 * K_BLOCKS * P * P * N_EDGES + 2 * P * P * N_EDGES
 
@@ -20,6 +21,12 @@ def tile_termedgempnnlayer_s_kernel(tc, base, h_ev, w1, b1, w3, b3, offs, out):
         tc.tile_pool(name="held", bufs=1) as held,
         tc.psum_pool(name="psum", bufs=1) as psum,
     ):
+        zeros = held.tile([P, CHUNK], BF16, name="zeros")
+        nc.vector.memset(zeros[:], 0.0)
+        warm_ps = psum.tile([P, CHUNK], F32, name="warm_ps")
+        for i in range(WARM_MATMULS):
+            nc.tensor.matmul(warm_ps[:], zeros[:, :P], zeros[:], start=True, stop=True)
+
         offsets = held.tile([P, N_EDGES // 16], U16, name="offsets")
         nc.sync.dma_start(offsets[:], offs)
 
@@ -28,8 +35,7 @@ def tile_termedgempnnlayer_s_kernel(tc, base, h_ev, w1, b1, w3, b3, offs, out):
         edges = []
         for k in range(K_BLOCKS):
             block = held.tile([P, N_EDGES], BF16, name=f"edges{k}")
-            queue = nc.sync if k % 2 == 0 else nc.scalar
-            queue.dma_start(block[:], h_ev[k * P : (k + 1) * P, :])
+            nc.sync.dma_start(block[:], h_ev[k * P : (k + 1) * P, :])
             edges.append(block)
         b1_sb = held.tile([P, 1], F32, name="b1_sb")
         nc.scalar.dma_start(b1_sb[:], b1)
@@ -46,20 +52,16 @@ def tile_termedgempnnlayer_s_kernel(tc, base, h_ev, w1, b1, w3, b3, offs, out):
         nc.sync.dma_start(window[:, :half], base[:, :half])
         nc.scalar.dma_start(window[:, half:], base[:, half:])
 
-        hid_ps = [psum.tile([P, CHUNK], F32, name=f"hid_ps{c}") for c in range(N_CHUNKS)]
-        for k in range(K_BLOCKS):
-            for c in range(N_CHUNKS):
-                nc.tensor.matmul(
-                    hid_ps[c][:],
-                    w1_sb[:, k, :],
-                    edges[k][:, c * CHUNK : (c + 1) * CHUNK],
-                    start=(k == 0),
-                    stop=(k == K_BLOCKS - 1),
-                )
         hid = []
         for c in range(N_CHUNKS):
+            cols = slice(c * CHUNK, (c + 1) * CHUNK)
+            hid_ps = psum.tile([P, CHUNK], F32, name=f"hid_ps{c}")
+            for k in range(K_BLOCKS):
+                nc.tensor.matmul(
+                    hid_ps[:], w1_sb[:, k, :], edges[k][:, cols], start=(k == 0), stop=(k == K_BLOCKS - 1)
+                )
             hid_c = held.tile([P, CHUNK], BF16, name=f"hid{c}")
-            nc.vector.tensor_scalar(hid_c[:], hid_ps[c][:], b1_sb[:, 0:1], 0.0, ADD, MAX)
+            nc.vector.tensor_scalar(hid_c[:], hid_ps[:], b1_sb[:, 0:1], 0.0, ADD, MAX)
             hid.append(hid_c)
 
         msg = held.tile([P, N_EDGES], F32, name="msg")

@@ -45,8 +45,7 @@ def tile_termedgempnnlayer_s_kernel(tc, base, h_ev, w1, b1, w3, b3, offs, out):
         nc.scalar.dma_start(b3_sb[:], b3)
 
         b3_wide = held.tile([P, N_EDGES], F32, name="b3_wide")
-        nc.gpsimd.memset(b3_wide[:], 0.0)
-        nc.gpsimd.tensor_scalar(b3_wide[:], b3_wide[:], 1.0, b3_sb[:, 0:1], MULT, ADD)
+        nc.gpsimd.tensor_scalar(b3_wide[:], b3_sb[:, 0:1].to_broadcast([P, N_EDGES]), 1.0, 0.0, MULT, ADD)
 
         window = held.tile([P, N_PLACES], F32, name="window")
         nc.sync.dma_start(window[:, :half], base[:, :half])

@@ -72,5 +72,4 @@ def tile_termedgempnnlayer_s_kernel(tc, base, h_ev, w1, b1, w3, b3, offs, out):
 
         nc.vector.tensor_tensor(window[:].indirect(offsets[:]), msg[:], b3_wide[:], ADD)
 
-        nc.sync.dma_start(out[:, :half], window[:, :half])
-        nc.scalar.dma_start(out[:, half:], window[:, half:])
+        nc.sync.dma_start(out, window[:])

@@ -12,11 +12,11 @@ FLOPS = 2 * K_BLOCKS * P * P * N_EDGES + 2 * P * P * N_EDGES
 
 BF16, F32, U16 = mybir.dt.bfloat16, mybir.dt.float32, mybir.dt.uint16
 ADD, MAX, MULT = mybir.AluOpType.add, mybir.AluOpType.max, mybir.AluOpType.mult
+RELU = mybir.ActivationFunctionType.Relu
 
 
 def tile_termedgempnnlayer_s_kernel(tc, base, h_ev, w1, b1, w3, b3, offs, out):
     nc = tc.nc
-    half = N_PLACES // 2
     with (
         tc.tile_pool(name="held", bufs=1) as held,
         tc.psum_pool(name="psum", bufs=1) as psum,
@@ -27,48 +27,47 @@ def tile_termedgempnnlayer_s_kernel(tc, base, h_ev, w1, b1, w3, b3, offs, out):
         for i in range(WARM_MATMULS):
             nc.tensor.matmul(warm_ps[:], zeros[:, :P], zeros[:], start=True, stop=True)
 
+        edges = h_ev.rearrange("(p k) j -> p k j", k=K_BLOCKS)
+        edges_01 = held.tile([P, 2, N_EDGES], BF16, name="edges_01")
+        nc.sync.dma_start(edges_01[:], edges[:, :2, :])
+        w1_sb = held.tile([P, K_BLOCKS, P], BF16, name="w1_sb")
+        nc.scalar.dma_start(w1_sb[:], w1.rearrange("(p k) h -> p k h", k=K_BLOCKS))
+        edges_2 = held.tile([P, N_EDGES], BF16, name="edges_2")
+        nc.scalar.dma_start(edges_2[:], edges[:, 2, :])
+        b1_sb = held.tile([P, 1], F32, name="b1_sb")
+        nc.sync.dma_start(b1_sb[:], b1)
+        w3_sb = held.tile([P, P], BF16, name="w3_sb")
+        nc.sync.dma_start(w3_sb[:], w3)
+        b3_sb = held.tile([P, 1], F32, name="b3_sb")
+        nc.sync.dma_start(b3_sb[:], b3)
         offsets = held.tile([P, N_EDGES // 16], U16, name="offsets")
         nc.sync.dma_start(offsets[:], offs)
-
-        w1_sb = held.tile([P, K_BLOCKS, P], BF16, name="w1_sb")
-        nc.scalar.dma_start(w1_sb[:], w1.rearrange("(k p) h -> p k h", p=P))
-        edges = []
-        for k in range(K_BLOCKS):
-            block = held.tile([P, N_EDGES], BF16, name=f"edges{k}")
-            nc.sync.dma_start(block[:], h_ev[k * P : (k + 1) * P, :])
-            edges.append(block)
-        b1_sb = held.tile([P, 1], F32, name="b1_sb")
-        nc.scalar.dma_start(b1_sb[:], b1)
-        w3_sb = held.tile([P, P], BF16, name="w3_sb")
-        nc.scalar.dma_start(w3_sb[:], w3)
-        b3_sb = held.tile([P, 1], F32, name="b3_sb")
-        nc.scalar.dma_start(b3_sb[:], b3)
+        window = held.tile([P, N_PLACES], F32, name="window")
+        nc.sync.dma_start(window[:], base)
+        early = held.tile([P, 1], BF16, name="early")
+        nc.scalar.activation(early[:], zeros[:, 0:1], RELU)
 
         b3_wide = held.tile([P, N_EDGES], F32, name="b3_wide")
         nc.gpsimd.tensor_scalar(b3_wide[:], b3_sb[:, 0:1].to_broadcast([P, N_EDGES]), 1.0, 0.0, MULT, ADD)
 
-        window = held.tile([P, N_PLACES], F32, name="window")
-        nc.sync.dma_start(window[:, :half], base[:, :half])
-        nc.scalar.dma_start(window[:, half:], base[:, half:])
-
-        hid = []
-        for c in range(N_CHUNKS):
-            cols = slice(c * CHUNK, (c + 1) * CHUNK)
-            hid_ps = psum.tile([P, CHUNK], F32, name=f"hid_ps{c}")
-            for k in range(K_BLOCKS):
+        chunks = [slice(c * CHUNK, (c + 1) * CHUNK) for c in range(N_CHUNKS)]
+        hid_ps = [psum.tile([P, CHUNK], F32, name=f"hid_ps{c}") for c in range(N_CHUNKS)]
+        blocks = [edges_01[:, 0, :], edges_01[:, 1, :], edges_2[:]]
+        for k, block in enumerate(blocks):
+            for c, cols in enumerate(chunks):
                 nc.tensor.matmul(
-                    hid_ps[:], w1_sb[:, k, :], edges[k][:, cols], start=(k == 0), stop=(k == K_BLOCKS - 1)
+                    hid_ps[c][:], w1_sb[:, k, :], block[:, cols], start=(k == 0), stop=(k == K_BLOCKS - 1)
                 )
-            hid_c = held.tile([P, CHUNK], BF16, name=f"hid{c}")
-            nc.vector.tensor_scalar(hid_c[:], hid_ps[:], b1_sb[:, 0:1], 0.0, ADD, MAX)
-            hid.append(hid_c)
+        hid = [held.tile([P, CHUNK], BF16, name=f"hid{c}") for c in range(N_CHUNKS)]
+        nc.vector.tensor_scalar(hid[0][:], hid_ps[0][:], b1_sb[:, 0:1], 0.0, ADD, MAX)
+        nc.scalar.activation(hid[1][:], hid_ps[1][:], RELU, bias=b1_sb[:, 0:1])
 
-        msg = held.tile([P, N_EDGES], F32, name="msg")
+        msg_ps = [psum.tile([P, CHUNK], F32, name=f"msg_ps{c}") for c in range(N_CHUNKS)]
         for c in range(N_CHUNKS):
-            cols = slice(c * CHUNK, (c + 1) * CHUNK)
-            msg_ps = psum.tile([P, CHUNK], F32, name=f"msg_ps{c}")
-            nc.tensor.matmul(msg_ps[:], w3_sb[:], hid[c][:], start=True, stop=True)
-            nc.vector.tensor_copy(msg[:, cols], msg_ps[:])
+            nc.tensor.matmul(msg_ps[c][:], w3_sb[:], hid[c][:], start=True, stop=True)
+        msg = held.tile([P, N_EDGES], F32, name="msg")
+        nc.vector.tensor_copy(msg[:, chunks[0]], msg_ps[0][:])
+        nc.scalar.copy(msg[:, chunks[1]], msg_ps[1][:])
 
         nc.vector.tensor_tensor(window[:].indirect(offsets[:]), msg[:], b3_wide[:], ADD)
 

@@ -4,6 +4,7 @@ P = 128
 N_EDGES = 512
 N_PLACES = 2048
 K_BLOCKS = 3
+BLOCK = 32
 N_CHUNKS = 2
 CHUNK = N_EDGES // N_CHUNKS
 WARM_MATMULS = 6
@@ -23,6 +24,8 @@ def tile_termedgempnnlayer_s_kernel(tc, base, h_ev, w1, b1, w3, b3, offs, out):
     ):
         zeros = held.tile([P, CHUNK], BF16, name="zeros")
         nc.vector.memset(zeros[:], 0.0)
+        bias_rows = held.tile([P, P], F32, name="bias_rows", align_bytes=64)
+        nc.vector.memset(bias_rows[:], 0.0)
         warm_ps = psum.tile([P, CHUNK], F32, name="warm_ps")
         for i in range(WARM_MATMULS):
             nc.tensor.matmul(warm_ps[:], zeros[:, :P], zeros[:], start=True, stop=True)
@@ -34,21 +37,24 @@ def tile_termedgempnnlayer_s_kernel(tc, base, h_ev, w1, b1, w3, b3, offs, out):
         nc.scalar.dma_start(w1_sb[:], w1.rearrange("(p k) h -> p k h", k=K_BLOCKS))
         edges_2 = held.tile([P, N_EDGES], BF16, name="edges_2")
         nc.scalar.dma_start(edges_2[:], edges[:, 2, :])
-        b1_sb = held.tile([P, 1], F32, name="b1_sb")
-        nc.sync.dma_start(b1_sb[:], b1)
         w3_sb = held.tile([P, P], BF16, name="w3_sb")
         nc.sync.dma_start(w3_sb[:], w3)
-        b3_sb = held.tile([P, 1], F32, name="b3_sb")
-        nc.sync.dma_start(b3_sb[:], b3)
         offsets = held.tile([P, N_EDGES // 16], U16, name="offsets")
         nc.sync.dma_start(offsets[:], offs)
+        nc.sync.dma_start(bias_rows[::BLOCK, :BLOCK], b1.rearrange("(q r) o -> q (r o)", r=BLOCK))
+        nc.sync.dma_start(bias_rows[::BLOCK, BLOCK : 2 * BLOCK], b3.rearrange("(q r) o -> q (r o)", r=BLOCK))
         window = held.tile([P, N_PLACES], F32, name="window")
         nc.sync.dma_start(window[:], base)
         early = held.tile([P, 1], BF16, name="early")
         nc.scalar.activation(early[:], zeros[:, 0:1], RELU)
 
+        bias_cols = held.tile([P, P], F32, name="bias_cols", align_bytes=64)
+        nc.vector.transpose(bias_cols[:], bias_rows[:])
+        b1_col = bias_cols[:, 0:1]
+        b3_col = bias_cols[:, BLOCK : BLOCK + 1]
+
         b3_wide = held.tile([P, N_EDGES], F32, name="b3_wide")
-        nc.gpsimd.tensor_scalar(b3_wide[:], b3_sb[:, 0:1].to_broadcast([P, N_EDGES]), 1.0, 0.0, MULT, ADD)
+        nc.gpsimd.tensor_scalar(b3_wide[:], b3_col.to_broadcast([P, N_EDGES]), 1.0, 0.0, MULT, ADD)
 
         chunks = [slice(c * CHUNK, (c + 1) * CHUNK) for c in range(N_CHUNKS)]
         hid_ps = [psum.tile([P, CHUNK], F32, name=f"hid_ps{c}") for c in range(N_CHUNKS)]
@@ -59,8 +65,8 @@ def tile_termedgempnnlayer_s_kernel(tc, base, h_ev, w1, b1, w3, b3, offs, out):
                     hid_ps[c][:], w1_sb[:, k, :], block[:, cols], start=(k == 0), stop=(k == K_BLOCKS - 1)
                 )
         hid = [held.tile([P, CHUNK], BF16, name=f"hid{c}") for c in range(N_CHUNKS)]
-        nc.vector.tensor_scalar(hid[0][:], hid_ps[0][:], b1_sb[:, 0:1], 0.0, ADD, MAX)
-        nc.scalar.activation(hid[1][:], hid_ps[1][:], RELU, bias=b1_sb[:, 0:1])
+        nc.vector.tensor_scalar(hid[0][:], hid_ps[0][:], b1_col, 0.0, ADD, MAX)
+        nc.scalar.activation(hid[1][:], hid_ps[1][:], RELU, bias=b1_col)
 
         msg_ps = [psum.tile([P, CHUNK], F32, name=f"msg_ps{c}") for c in range(N_CHUNKS)]
         for c in range(N_CHUNKS):

@@ -12,7 +12,7 @@ WARM_MATMULS = 6
 FLOPS = 2 * K_BLOCKS * P * P * N_EDGES + 2 * P * P * N_EDGES
 
 BF16, F32, U16 = mybir.dt.bfloat16, mybir.dt.float32, mybir.dt.uint16
-ADD, MAX, MULT = mybir.AluOpType.add, mybir.AluOpType.max, mybir.AluOpType.mult
+ADD, MAX = mybir.AluOpType.add, mybir.AluOpType.max
 RELU = mybir.ActivationFunctionType.Relu
 
 
@@ -32,17 +32,17 @@ def tile_termedgempnnlayer_s_kernel(tc, base, h_ev, w1, b1, w3, b3, offs, out):
 
         edges = h_ev.rearrange("(p k) j -> p k j", k=K_BLOCKS)
         edges_01 = held.tile([P, 2, N_EDGES], BF16, name="edges_01")
-        nc.sync.dma_start(edges_01[:], edges[:, :2, :])
+        nc.scalar.dma_start(edges_01[:], edges[:, :2, :])
         w1_sb = held.tile([P, K_BLOCKS, P], BF16, name="w1_sb")
-        nc.scalar.dma_start(w1_sb[:], w1.rearrange("(p k) h -> p k h", k=K_BLOCKS))
+        nc.sync.dma_start(w1_sb[:], w1.rearrange("(p k) h -> p k h", k=K_BLOCKS))
+        nc.sync.dma_start(bias_rows[::BLOCK, :BLOCK], b1.rearrange("(q r) o -> q (r o)", r=BLOCK))
+        nc.sync.dma_start(bias_rows[::BLOCK, BLOCK : 2 * BLOCK], b3.rearrange("(q r) o -> q (r o)", r=BLOCK))
         edges_2 = held.tile([P, N_EDGES], BF16, name="edges_2")
-        nc.scalar.dma_start(edges_2[:], edges[:, 2, :])
+        nc.sync.dma_start(edges_2[:], edges[:, 2, :])
         w3_sb = held.tile([P, P], BF16, name="w3_sb")
         nc.sync.dma_start(w3_sb[:], w3)
         offsets = held.tile([P, N_EDGES // 16], U16, name="offsets")
         nc.sync.dma_start(offsets[:], offs)
-        nc.sync.dma_start(bias_rows[::BLOCK, :BLOCK], b1.rearrange("(q r) o -> q (r o)", r=BLOCK))
-        nc.sync.dma_start(bias_rows[::BLOCK, BLOCK : 2 * BLOCK], b3.rearrange("(q r) o -> q (r o)", r=BLOCK))
         window = held.tile([P, N_PLACES], F32, name="window")
         nc.sync.dma_start(window[:], base)
         early = held.tile([P, 1], BF16, name="early")
@@ -54,7 +54,7 @@ def tile_termedgempnnlayer_s_kernel(tc, base, h_ev, w1, b1, w3, b3, offs, out):
         b3_col = bias_cols[:, BLOCK : BLOCK + 1]
 
         b3_wide = held.tile([P, N_EDGES], F32, name="b3_wide")
-        nc.gpsimd.tensor_scalar(b3_wide[:], b3_col.to_broadcast([P, N_EDGES]), 1.0, 0.0, MULT, ADD)
+        nc.vector.tensor_copy(b3_wide[:], b3_col.to_broadcast([P, N_EDGES]))
 
         chunks = [slice(c * CHUNK, (c + 1) * CHUNK) for c in range(N_CHUNKS)]
         hid_ps = [psum.tile([P, CHUNK], F32, name=f"hid_ps{c}") for c in range(N_CHUNKS)]

@@ -24,7 +24,7 @@ def tile_termedgempnnlayer_s_kernel(tc, base, h_ev, w1, b1, w3, b3, offs, out):
     ):
         zeros = held.tile([P, CHUNK], BF16, name="zeros")
         nc.vector.memset(zeros[:], 0.0)
-        bias_rows = held.tile([P, P], F32, name="bias_rows", align_bytes=64)
+        bias_rows = held.tile([P, BLOCK], F32, name="bias_rows", align_bytes=64)
         nc.vector.memset(bias_rows[:], 0.0)
         warm_ps = psum.tile([P, CHUNK], F32, name="warm_ps")
         for i in range(WARM_MATMULS):
@@ -35,23 +35,23 @@ def tile_termedgempnnlayer_s_kernel(tc, base, h_ev, w1, b1, w3, b3, offs, out):
         nc.scalar.dma_start(edges_01[:], edges[:, :2, :])
         w1_sb = held.tile([P, K_BLOCKS, P], BF16, name="w1_sb")
         nc.sync.dma_start(w1_sb[:], w1.rearrange("(p k) h -> p k h", k=K_BLOCKS))
-        nc.sync.dma_start(bias_rows[::BLOCK, :BLOCK], b1.rearrange("(q r) o -> q (r o)", r=BLOCK))
-        nc.sync.dma_start(bias_rows[::BLOCK, BLOCK : 2 * BLOCK], b3.rearrange("(q r) o -> q (r o)", r=BLOCK))
         edges_2 = held.tile([P, N_EDGES], BF16, name="edges_2")
         nc.sync.dma_start(edges_2[:], edges[:, 2, :])
         w3_sb = held.tile([P, P], BF16, name="w3_sb")
         nc.sync.dma_start(w3_sb[:], w3)
         offsets = held.tile([P, N_EDGES // 16], U16, name="offsets")
         nc.sync.dma_start(offsets[:], offs)
+        nc.sync.dma_start(bias_rows[0::BLOCK, :], b1.rearrange("(q r) o -> q (r o)", r=BLOCK))
+        nc.sync.dma_start(bias_rows[1::BLOCK, :], b3.rearrange("(q r) o -> q (r o)", r=BLOCK))
         window = held.tile([P, N_PLACES], F32, name="window")
         nc.sync.dma_start(window[:], base)
         early = held.tile([P, 1], BF16, name="early")
         nc.scalar.activation(early[:], zeros[:, 0:1], RELU)
 
-        bias_cols = held.tile([P, P], F32, name="bias_cols", align_bytes=64)
+        bias_cols = held.tile([P, BLOCK], F32, name="bias_cols", align_bytes=64)
         nc.vector.transpose(bias_cols[:], bias_rows[:])
         b1_col = bias_cols[:, 0:1]
-        b3_col = bias_cols[:, BLOCK : BLOCK + 1]
+        b3_col = bias_cols[:, 1:2]
 
         b3_wide = held.tile([P, N_EDGES], F32, name="b3_wide")
         nc.vector.tensor_copy(b3_wide[:], b3_col.to_broadcast([P, N_EDGES]))
@@ -65,15 +65,15 @@ def tile_termedgempnnlayer_s_kernel(tc, base, h_ev, w1, b1, w3, b3, offs, out):
                     hid_ps[c][:], w1_sb[:, k, :], block[:, cols], start=(k == 0), stop=(k == K_BLOCKS - 1)
                 )
         hid = [held.tile([P, CHUNK], BF16, name=f"hid{c}") for c in range(N_CHUNKS)]
-        nc.vector.tensor_scalar(hid[0][:], hid_ps[0][:], b1_col, 0.0, ADD, MAX)
-        nc.scalar.activation(hid[1][:], hid_ps[1][:], RELU, bias=b1_col)
+        nc.scalar.activation(hid[0][:], hid_ps[0][:], RELU, bias=b1_col)
+        nc.vector.tensor_scalar(hid[1][:], hid_ps[1][:], b1_col, 0.0, ADD, MAX)
 
         msg_ps = [psum.tile([P, CHUNK], F32, name=f"msg_ps{c}") for c in range(N_CHUNKS)]
         for c in range(N_CHUNKS):
             nc.tensor.matmul(msg_ps[c][:], w3_sb[:], hid[c][:], start=True, stop=True)
         msg = held.tile([P, N_EDGES], F32, name="msg")
-        nc.vector.tensor_copy(msg[:, chunks[0]], msg_ps[0][:])
-        nc.scalar.copy(msg[:, chunks[1]], msg_ps[1][:])
+        nc.scalar.copy(msg[:, chunks[0]], msg_ps[0][:])
+        nc.vector.tensor_copy(msg[:, chunks[1]], msg_ps[1][:])
 
         nc.vector.tensor_tensor(window[:].indirect(offsets[:]), msg[:], b3_wide[:], ADD)
 

@@ -5,6 +5,7 @@ N_EDGES = 512
 N_PLACES = 2048
 K_BLOCKS = 3
 BLOCK = 32
+LINE = 256
 N_CHUNKS = 2
 CHUNK = N_EDGES // N_CHUNKS
 WARM_MATMULS = 6
@@ -24,26 +25,26 @@ def tile_termedgempnnlayer_s_kernel(tc, base, h_ev, w1, b1, w3, b3, offs, out):
     ):
         zeros = held.tile([P, CHUNK], BF16, name="zeros")
         nc.vector.memset(zeros[:], 0.0)
-        bias_rows = held.tile([P, BLOCK], F32, name="bias_rows", align_bytes=64)
+        bias_rows = held.tile([P, BLOCK], F32, name="bias_rows", align_bytes=LINE)
         nc.vector.memset(bias_rows[:], 0.0)
         warm_ps = psum.tile([P, CHUNK], F32, name="warm_ps")
         for i in range(WARM_MATMULS):
             nc.tensor.matmul(warm_ps[:], zeros[:, :P], zeros[:], start=True, stop=True)
 
         edges = h_ev.rearrange("(p k) j -> p k j", k=K_BLOCKS)
-        edges_01 = held.tile([P, 2, N_EDGES], BF16, name="edges_01")
+        edges_01 = held.tile([P, 2, N_EDGES], BF16, name="edges_01", align_bytes=LINE)
         nc.scalar.dma_start(edges_01[:], edges[:, :2, :])
-        w1_sb = held.tile([P, K_BLOCKS, P], BF16, name="w1_sb")
+        w1_sb = held.tile([P, K_BLOCKS, P], BF16, name="w1_sb", align_bytes=LINE)
         nc.sync.dma_start(w1_sb[:], w1.rearrange("(p k) h -> p k h", k=K_BLOCKS))
-        edges_2 = held.tile([P, N_EDGES], BF16, name="edges_2")
+        edges_2 = held.tile([P, N_EDGES], BF16, name="edges_2", align_bytes=LINE)
         nc.sync.dma_start(edges_2[:], edges[:, 2, :])
-        w3_sb = held.tile([P, P], BF16, name="w3_sb")
+        w3_sb = held.tile([P, P], BF16, name="w3_sb", align_bytes=LINE)
         nc.sync.dma_start(w3_sb[:], w3)
-        offsets = held.tile([P, N_EDGES // 16], U16, name="offsets")
+        offsets = held.tile([P, N_EDGES // 16], U16, name="offsets", align_bytes=LINE)
         nc.sync.dma_start(offsets[:], offs)
         nc.sync.dma_start(bias_rows[0::BLOCK, :], b1.rearrange("(q r) o -> q (r o)", r=BLOCK))
         nc.sync.dma_start(bias_rows[1::BLOCK, :], b3.rearrange("(q r) o -> q (r o)", r=BLOCK))
-        window = held.tile([P, N_PLACES], F32, name="window")
+        window = held.tile([P, N_PLACES], F32, name="window", align_bytes=LINE)
         nc.sync.dma_start(window[:], base)
         early = held.tile([P, 1], BF16, name="early")
         nc.scalar.activation(early[:], zeros[:, 0:1], RELU)

import concourse.mybir as mybir

P = 128
N_EDGES = 512
N_PLACES = 2048
K_BLOCKS = 3
BLOCK = 32
LINE = 256
N_CHUNKS = 2
CHUNK = N_EDGES // N_CHUNKS
WARM_MATMULS = 6

FLOPS = 2 * K_BLOCKS * P * P * N_EDGES + 2 * P * P * N_EDGES

BF16, F32, U16 = mybir.dt.bfloat16, mybir.dt.float32, mybir.dt.uint16
ADD, MAX = mybir.AluOpType.add, mybir.AluOpType.max
RELU = mybir.ActivationFunctionType.Relu


def tile_termedgempnnlayer_s_kernel(tc, base, h_ev, w1, b1, w3, b3, offs, out):
    nc = tc.nc
    with (
        tc.tile_pool(name="held", bufs=1) as held,
        tc.psum_pool(name="psum", bufs=1) as psum,
    ):
        zeros = held.tile([P, CHUNK], BF16, name="zeros")
        nc.vector.memset(zeros[:], 0.0)
        bias_rows = held.tile([P, BLOCK], F32, name="bias_rows", align_bytes=LINE)
        nc.vector.memset(bias_rows[:], 0.0)
        warm_ps = psum.tile([P, CHUNK], F32, name="warm_ps")
        for i in range(WARM_MATMULS):
            nc.tensor.matmul(warm_ps[:], zeros[:, :P], zeros[:], start=True, stop=True)

        edges = h_ev.rearrange("(p k) j -> p k j", k=K_BLOCKS)
        edges_01 = held.tile([P, 2, N_EDGES], BF16, name="edges_01", align_bytes=LINE)
        nc.scalar.dma_start(edges_01[:], edges[:, :2, :])
        w1_sb = held.tile([P, K_BLOCKS, P], BF16, name="w1_sb", align_bytes=LINE)
        nc.sync.dma_start(w1_sb[:], w1.rearrange("(p k) h -> p k h", k=K_BLOCKS))
        edges_2 = held.tile([P, N_EDGES], BF16, name="edges_2", align_bytes=LINE)
        nc.sync.dma_start(edges_2[:], edges[:, 2, :])
        w3_sb = held.tile([P, P], BF16, name="w3_sb", align_bytes=LINE)
        nc.sync.dma_start(w3_sb[:], w3)
        offsets = held.tile([P, N_EDGES // 16], U16, name="offsets", align_bytes=LINE)
        nc.sync.dma_start(offsets[:], offs)
        nc.sync.dma_start(bias_rows[0::BLOCK, :], b1.rearrange("(q r) o -> q (r o)", r=BLOCK))
        nc.sync.dma_start(bias_rows[1::BLOCK, :], b3.rearrange("(q r) o -> q (r o)", r=BLOCK))
        window = held.tile([P, N_PLACES], F32, name="window", align_bytes=LINE)
        nc.sync.dma_start(window[:], base)
        early = held.tile([P, 1], BF16, name="early")
        nc.scalar.activation(early[:], zeros[:, 0:1], RELU)

        bias_cols = held.tile([P, BLOCK], F32, name="bias_cols", align_bytes=64)
        nc.vector.transpose(bias_cols[:], bias_rows[:])
        b1_col = bias_cols[:, 0:1]
        b3_col = bias_cols[:, 1:2]

        b3_wide = held.tile([P, N_EDGES], F32, name="b3_wide")
        nc.vector.tensor_copy(b3_wide[:], b3_col.to_broadcast([P, N_EDGES]))

        chunks = [slice(c * CHUNK, (c + 1) * CHUNK) for c in range(N_CHUNKS)]
        hid_ps = [psum.tile([P, CHUNK], F32, name=f"hid_ps{c}") for c in range(N_CHUNKS)]
        blocks = [edges_01[:, 0, :], edges_01[:, 1, :], edges_2[:]]
        for k, block in enumerate(blocks):
            for c, cols in enumerate(chunks):
                nc.tensor.matmul(
                    hid_ps[c][:], w1_sb[:, k, :], block[:, cols], start=(k == 0), stop=(k == K_BLOCKS - 1)
                )
        hid = [held.tile([P, CHUNK], BF16, name=f"hid{c}") for c in range(N_CHUNKS)]
        nc.scalar.activation(hid[0][:], hid_ps[0][:], RELU, bias=b1_col)
        nc.vector.tensor_scalar(hid[1][:], hid_ps[1][:], b1_col, 0.0, ADD, MAX)

        msg_ps = [psum.tile([P, CHUNK], F32, name=f"msg_ps{c}") for c in range(N_CHUNKS)]
        for c in range(N_CHUNKS):
            nc.tensor.matmul(msg_ps[c][:], w3_sb[:], hid[c][:], start=True, stop=True)
        msg = held.tile([P, N_EDGES], F32, name="msg")
        nc.scalar.copy(msg[:, chunks[0]], msg_ps[0][:])
        nc.vector.tensor_copy(msg[:, chunks[1]], msg_ps[1][:])

        nc.vector.tensor_tensor(window[:].indirect(offsets[:]), msg[:], b3_wide[:], ADD)

        nc.sync.dma_start(out, window[:])
